import numpy as np
import ml_dtypes


def mxq(x, axis, fmt="e4m3"):
    dtype, down = {"e4m3": (ml_dtypes.float8_e4m3fn, 7), "e5m2": (ml_dtypes.float8_e5m2, 14)}[fmt]
    v = np.moveaxis(np.asarray(x, np.float32).astype(ml_dtypes.bfloat16).astype(np.float64), axis, -1)
    blocks = v.reshape(v.shape[:-1] + (-1, 32))
    amax = np.abs(blocks).max(-1, keepdims=True)
    byte = np.maximum(np.where(amax > 0, np.frexp(amax)[1] - 1 + 127, 0) - down, 1)
    scale = np.exp2(byte - 127.0)
    codes = (blocks / scale).astype(np.float32).astype(dtype).astype(np.float64)
    return np.moveaxis((codes * scale).reshape(v.shape), -1, axis)


WIDE = False


def mx_kscale(k):
    if not WIDE:
        return np.ones(k)
    levels = np.array([10, -10, 5, -5, 0])
    a = np.random.permutation(np.resize(levels, k // 512 * 4)).reshape(k // 512, 4)
    idx = np.arange(k)
    return np.exp2(a[idx // 512, idx % 128 // 32])


BF16 = ml_dtypes.bfloat16


def bf(x):
    return np.asarray(x, np.float32).astype(BF16)


def f64(x):
    return np.asarray(x).astype(np.float64)


B, N, D0, D1, D2, D3 = 32, 128, 1024, 1024, 512, 1024
EPS = 1e-5


def batch_norm(x, g, b):
    mean = x.mean(axis=(0, 1))
    var = np.square(x - mean).mean(axis=(0, 1))
    return (x - mean) * (1.0 / np.sqrt(var + EPS)) * g + b


def setup_inputs():
    s = mx_kscale(D0)
    feats = np.random.standard_normal((B, N, D0)) * np.exp(0.4 * np.random.standard_normal(D0)) + 0.5 * np.random.standard_normal(D0)
    return {"set_feats": bf(feats),
            "g0": bf((1.0 + 0.2 * np.random.standard_normal(D0)) * s),
            "b0": bf(0.2 * np.random.standard_normal(D0) * s),
            "W0": bf(np.random.standard_normal((D1, D0)) / np.sqrt(D0) / s),
            "c0": bf(0.3 * np.random.standard_normal(D1)),
            "g1": bf(1.0 + 0.2 * np.random.standard_normal(D1)),
            "b1": bf(0.2 * np.random.standard_normal(D1))}


def reference(set_feats, g0, b0, W0, c0, g1, b1):
    x0 = batch_norm(f64(set_feats), f64(g0), f64(b0))
    h0 = np.maximum((mxq(x0, 2, "e4m3") @ mxq(f64(W0), 1, "e4m3").T) + f64(c0), 0.0)
    return batch_norm(h0, f64(g1), f64(b1))

@@ -1,0 +1,279 @@
+from contextlib import ExitStack
+
+import concourse.mybir as mybir
+from concourse.masks import make_identity
+
+F32 = mybir.dt.float32
+BF16 = mybir.dt.bfloat16
+U32 = mybir.dt.uint32
+U8 = mybir.dt.uint8
+FP8X4 = mybir.dt.float8_e4m3fn_x4
+ACT = mybir.ActivationFunctionType
+ALU = mybir.AluOpType
+AX = mybir.AxisListType
+
+P = 128
+ROWS = 4096
+K = 1024
+DOUT = 1024
+RT = ROWS // P
+KB = K // P
+MT = DOUT // P
+EPS = 1e-5
+FLOPS = 2 * ROWS * K * DOUT
+
+KB_V = 6
+N_ONES = 32
+S_REGROUP = {0: (1, 2, 3), 1: (1, 2, 3), 2: (1, 2, 3), 3: (1, 3)}
+V_EVAC = (1, 4, 6)
+STORE_GROUPS = ((0, 1), (2, 3), (4, 5), (6,), (7,))
+
+
+def tile_settransform_pa_t_kernel(tc, set_feats, g0, b0, W0, c0, g1, b1, out):
+    nc = tc.nc
+    x_v = set_feats.flatten_outer_dims().rearrange("(p j) k -> p j k", j=RT)
+    out_v = out.flatten_outer_dims().rearrange("(p j) d -> p j d", j=RT)
+    w_v = W0.rearrange("(m p) k -> p m k", p=P)
+
+    with ExitStack() as ctx:
+        const = ctx.enter_context(tc.tile_pool(name="const", bufs=1))
+        big = ctx.enter_context(tc.tile_pool(name="big", bufs=4))
+        small = ctx.enter_context(tc.tile_pool(name="small", bufs=3))
+        ps_t = ctx.enter_context(tc.psum_pool(name="ps_t", bufs=4))
+        ps_m = ctx.enter_context(tc.psum_pool(name="ps_m", bufs=4))
+
+        eps_t = const.tile([P, 1], F32, name="eps_t")
+        nc.vector.memset(eps_t[:], EPS)
+        warm = const.tile([P, 1], F32, name="warm")
+        nc.scalar.activation(out=warm[:], in_=eps_t[:], func=ACT.Sqrt)
+
+        ident_bf = const.tile([P, P], BF16, name="ident_bf")
+        make_identity(nc, ident_bf[:])
+        ident_f = const.tile([P, P], F32, name="ident_f")
+        make_identity(nc, ident_f[:])
+        ones_bf = const.tile([P, N_ONES], BF16, name="ones_bf")
+        nc.vector.memset(ones_bf[:], 1.0)
+
+        praw = const.tile([P, P], BF16, name="praw")
+        nc.vector.memset(praw[:], 0.0)
+        for i, v in enumerate((g0, b0, c0, g1, b1)):
+            nc.scalar.dma_start(out=praw[8 * i : 8 * i + 8, :], in_=v.rearrange("(j p) -> j p", p=P))
+        pps = ps_t.tile([P, P], BF16, name="pps", tag="tp")
+        nc.tensor.transpose(pps[:], praw[:], ident_bf[:])
+        par = const.tile([P, 40], F32, name="par")
+        nc.vector.tensor_copy(out=par[:], in_=pps[:, 0:40])
+        gpair = const.tile([P, MT, 2], F32, name="gpair")
+        nc.vector.tensor_copy(out=gpair[:, :, 0], in_=par[:, 24:32])
+        nc.vector.tensor_scalar(out=gpair[:, :, 1], in0=par[:, 24:32], scalar1=-1.0, scalar2=None, op0=ALU.mult)
+
+        xq = [const.tile([P, 2, 1024], U32, name="xq%d" % q, align_bytes=64) for q in range(4)]
+        xsc = [const.tile([P, 2, 1024], U8, name="xsc%d" % q, align_bytes=64) for q in range(4)]
+        wq = const.tile([P, 2, DOUT], U32, name="wq", align_bytes=64)
+        wsc = const.tile([P, 2, DOUT], U8, name="wsc", align_bytes=64)
+        st0 = const.tile([P, KB_V, 8, 6], F32, name="st0")
+        mv0 = const.tile([P, KB, 2], F32, name="mv0")
+        n_s = KB - KB_V
+        nmu = const.tile([P, n_s], F32, name="nmu")
+        sq = const.tile([P, n_s, 4], F32, name="sq")
+
+        with ExitStack() as actx:
+            xpool = actx.enter_context(tc.tile_pool(name="xpool", bufs=4))
+            wpool = actx.enter_context(tc.tile_pool(name="wpool", bufs=1))
+            gpool = actx.enter_context(tc.tile_pool(name="gpool", bufs=3))
+            jpool = actx.enter_context(tc.tile_pool(name="jpool", bufs=2))
+
+            xT = [big.tile([P, KB, 1024], BF16, name="xT%d" % q, tag="big") for q in range(4)]
+            w_sb = wpool.tile([P, MT, K], BF16, name="w_sb")
+            wT = wpool.tile([P, KB, DOUT], BF16, name="wT")
+            wg = wpool.tile([P, 2, DOUT, 4], BF16, name="wg", align_bytes=64)
+            sums = [ps_m.tile([P, N_ONES], F32, name="sums%d" % i, tag="acc") for i in range(n_s)]
+            first = ps_m.tile([P, n_s, N_ONES], F32, name="first", tag="acc")
+
+            def w_tile(m):
+                for hk in range(2):
+                    pt = ps_t.tile([P, 4, P], BF16, name="ptw", tag="tp")
+                    for t in range(4):
+                        kb = 4 * hk + t
+                        nc.tensor.transpose(pt[:, t, :], w_sb[:, m, kb * P : (kb + 1) * P], ident_bf[:])
+                    nc.scalar.copy(out=wT[:, 4 * hk : 4 * hk + 4, m * P : (m + 1) * P], in_=pt[:])
+
+            for c in range(8):
+                x_sb = xpool.tile([P, 4, K], BF16, name="x_sb", tag="x_sb")
+                nc.sync.dma_start(out=x_sb[:], in_=x_v[:, 4 * c : 4 * c + 4, :])
+                if c == 3:
+                    nc.sync.dma_start(out=w_sb[:], in_=w_v)
+                base = (c % 2) * 512
+                if c == 0:
+                    for i in range(n_s):
+                        kb = KB_V + i
+                        nc.tensor.matmul(
+                            out=first[:, i, :], lhsT=x_sb[:, 0, kb * P : (kb + 1) * P], rhs=ones_bf[:],
+                            start=True, stop=True,
+                        )
+                    nc.scalar.activation(out=nmu[:], in_=first[:, :, 0], func=ACT.Copy, scale=-1.0 / P)
+                for kb in range(KB):
+                    pt = ps_t.tile([P, 4, P], BF16, name="pt", tag="tp")
+                    for jj in range(4):
+                        nc.tensor.transpose(pt[:, jj, :], x_sb[:, jj, kb * P : (kb + 1) * P], ident_bf[:])
+                    dst = xT[c // 2][:, kb, base : base + 512]
+                    nc.scalar.copy(out=dst, in_=pt[:].rearrange("p j r -> p (j r)"))
+                    if kb < KB_V:
+                        nc.vector.bn_stats(out=st0[:, kb, c, :], in_=dst)
+                    else:
+                        for jj in range(4):
+                            nc.tensor.matmul(
+                                out=sums[kb - KB_V][:], lhsT=x_sb[:, jj, kb * P : (kb + 1) * P], rhs=ones_bf[:],
+                                start=(c == 0 and jj == 0), stop=(c == 7 and jj == 3),
+                            )
+                if c % 2 == 1:
+                    for i in range(n_s):
+                        junk = jpool.tile([P, 1024], BF16, name="junk", tag="junk")
+                        nc.scalar.activation(
+                            out=junk[:], in_=xT[c // 2][:, KB_V + i, :], func=ACT.Square,
+                            bias=nmu[:, i : i + 1], scale=1.0, accum_out=sq[:, i, c // 2 : c // 2 + 1],
+                        )
+                if c >= 4:
+                    w_tile(2 * (c - 4))
+                    w_tile(2 * (c - 4) + 1)
+                    if c % 2 == 1:
+                        lo = (c - 5) * 256
+                        for g in range(2):
+                            nc.gpsimd.tensor_scalar(
+                                out=wg[:, g, lo : lo + 512, :],
+                                in0=wT[:, 4 * g : 4 * g + 4, lo : lo + 512].rearrange("p t d -> p d t"),
+                                scalar1=1.0, scalar2=0.0, op0=ALU.mult, op1=ALU.add,
+                            )
+
+            for g in range(2):
+                nc.vector.quantize_mx(
+                    out=wq[:, g, :].bitcast(FP8X4),
+                    scales=wsc[:, g, :],
+                    in_=wg[:, g, :, :].rearrange("p d t -> p (d t)"),
+                )
+
+            for kb in range(KB_V):
+                nc.vector.bn_aggr(out=mv0[:, kb, :], in_=st0[:, kb, :, :].rearrange("p c s -> p (c s)"))
+            for i in range(n_s):
+                nc.vector.tensor_scalar(
+                    out=mv0[:, KB_V + i, 0:1], in0=sums[i][:, 0:1], scalar1=1.0 / ROWS, scalar2=None, op0=ALU.mult
+                )
+            sqs = const.tile([P, n_s], F32, name="sqs")
+            nc.vector.tensor_reduce(out=sqs[:], in_=sq[:], axis=AX.X, op=ALU.add)
+            dl = const.tile([P, n_s], F32, name="dl")
+            nc.vector.tensor_tensor(out=dl[:], in0=mv0[:, KB_V:KB, 0], in1=nmu[:], op=ALU.add)
+            dl2 = const.tile([P, n_s], F32, name="dl2")
+            nc.vector.tensor_tensor(out=dl2[:], in0=dl[:], in1=dl[:], op=ALU.mult)
+            nc.vector.scalar_tensor_tensor(
+                out=mv0[:, KB_V:KB, 1], in0=sqs[:], scalar=1.0 / ROWS, in1=dl2[:], op0=ALU.mult, op1=ALU.subtract
+            )
+            sd0 = const.tile([P, KB], F32, name="sd0")
+            nc.scalar.activation(out=sd0[:], in_=mv0[:, :, 1], func=ACT.Sqrt, bias=eps_t[:, 0:1], scale=1.0)
+            r0 = const.tile([P, KB], F32, name="r0")
+            nc.vector.reciprocal(out=r0[:], in_=sd0[:])
+            a0 = const.tile([P, KB], F32, name="a0")
+            nc.vector.tensor_tensor(out=a0[:], in0=r0[:], in1=par[:, 0:8], op=ALU.mult)
+            ma0 = const.tile([P, KB], F32, name="ma0")
+            nc.vector.tensor_tensor(out=ma0[:], in0=mv0[:, :, 0], in1=a0[:], op=ALU.mult)
+            nd0 = const.tile([P, KB], F32, name="nd0")
+            nc.vector.tensor_tensor(out=nd0[:], in0=ma0[:], in1=par[:, 8:16], op=ALU.subtract)
+
+            for q in range(4):
+                for kb in range(KB):
+                    nc.vector.tensor_scalar(
+                        out=xT[q][:, kb, :], in0=xT[q][:, kb, :],
+                        scalar1=a0[:, kb : kb + 1], scalar2=nd0[:, kb : kb + 1],
+                        op0=ALU.mult, op1=ALU.subtract,
+                    )
+                for g in range(2):
+                    gr = gpool.tile([P, 1024, 4], BF16, name="gr", tag="gr", align_bytes=64)
+                    for hf in range(2):
+                        src = xT[q][:, 4 * g : 4 * g + 4, hf * 512 : (hf + 1) * 512]
+                        dst = gr[:, hf * 512 : (hf + 1) * 512, :]
+                        dst_v = dst.rearrange("p (c i) t -> p c t i", i=4)
+                        src_v = src.rearrange("p t (c i) -> p c t i", i=4)
+                        if 2 * g + hf in S_REGROUP[q]:
+                            nc.scalar.copy(out=dst_v, in_=src_v)
+                        else:
+                            nc.vector.tensor_copy(out=dst_v, in_=src_v)
+                    nc.vector.quantize_mx(
+                        out=xq[q][:, g, :].bitcast(FP8X4),
+                        scales=xsc[q][:, g, :],
+                        in_=gr[:].rearrange("p r t -> p (r t)"),
+                    )
+
+        with ExitStack() as bctx:
+            spool = bctx.enter_context(tc.tile_pool(name="spool", bufs=2))
+            h = {}
+            st1 = {}
+            stage = {}
+
+            def mx_tile(m):
+                h[m] = big.tile([P, ROWS], F32, name="h%d" % m, tag="big")
+                st1[m] = small.tile([P, 8, 6], F32, name="st1", tag="st1")
+                for c in range(8):
+                    acc = ps_m.tile([P, 512], F32, name="acc", tag="acc")
+                    q, hf = c // 2, c % 2
+                    for g in range(2):
+                        nc.tensor.matmul_mx(
+                            out=acc[:],
+                            lhsT=wq[:, g, m * P : (m + 1) * P].bitcast(FP8X4),
+                            lhsT_scale=wsc[:, g, m * P : (m + 1) * P],
+                            rhs=xq[q][:, g, hf * 512 : (hf + 1) * 512].bitcast(FP8X4),
+                            rhs_scale=xsc[q][:, g, hf * 512 : (hf + 1) * 512],
+                            start=(g == 0),
+                            stop=(g == 1),
+                        )
+                    nc.scalar.activation(
+                        out=h[m][:, c * 512 : (c + 1) * 512], in_=acc[:], func=ACT.Relu,
+                        bias=par[:, 16 + m : 17 + m], scale=1.0,
+                    )
+                    nc.vector.bn_stats(out=st1[m][:, c, :], in_=h[m][:, c * 512 : (c + 1) * 512])
+
+            def finish_tile(m):
+                mv = small.tile([P, 2], F32, name="mv", tag="mv")
+                nc.vector.bn_aggr(out=mv[:], in_=st1[m][:].rearrange("p c s -> p (c s)"))
+                sd = small.tile([P, 1], F32, name="sd", tag="sd")
+                nc.scalar.activation(out=sd[:], in_=mv[:, 1:2], func=ACT.Sqrt, bias=eps_t[:, 0:1], scale=1.0)
+                r1 = small.tile([P, 1], F32, name="r1", tag="r1")
+                nc.vector.reciprocal(out=r1[:], in_=sd[:])
+                a1 = small.tile([P, 2], F32, name="a1", tag="a1")
+                nc.vector.tensor_scalar(out=a1[:], in0=gpair[:, m, :], scalar1=r1[:, 0:1], scalar2=None, op0=ALU.mult)
+                d1 = small.tile([P, 1], F32, name="d1", tag="d1")
+                nc.vector.scalar_tensor_tensor(
+                    out=d1[:], in0=mv[:, 0:1], scalar=a1[:, 1:2], in1=par[:, 32 + m : 33 + m],
+                    op0=ALU.mult, op1=ALU.add,
+                )
+                for s in range(4):
+                    nc.gpsimd.tensor_scalar(
+                        out=h[m][:, s * 1024 : (s + 1) * 1024], in0=h[m][:, s * 1024 : (s + 1) * 1024],
+                        scalar1=a1[:, 0:1], scalar2=d1[:, 0:1], op0=ALU.mult, op1=ALU.add,
+                    )
+                grp = [gr_ for gr_ in STORE_GROUPS if m in gr_][0]
+                gi = grp.index(m)
+                width = len(grp) * P
+                if gi == 0:
+                    stage[grp] = spool.tile([P, RT, width], F32, name="stage", tag="stage")
+                stg = stage[grp]
+                for c in range(8):
+                    pt = ps_t.tile([P, 4, P], F32, name="pto", tag="tp")
+                    for jj in range(4):
+                        j = 4 * c + jj
+                        nc.tensor.transpose(pt[:, jj, :], h[m][:, j * P : (j + 1) * P], ident_f[:])
+                    dst = stg[:, 4 * c : 4 * c + 4, gi * P : (gi + 1) * P]
+                    if c in V_EVAC:
+                        nc.vector.tensor_copy(out=dst, in_=pt[:])
+                    else:
+                        nc.scalar.copy(out=dst, in_=pt[:])
+                    if gi == len(grp) - 1 and c % 2 == 1:
+                        s = c // 2
+                        nc.sync.dma_start(
+                            out=out_v[:, 8 * s : 8 * s + 8, grp[0] * P : grp[0] * P + width],
+                            in_=stg[:, 8 * s : 8 * s + 8, :],
+                        )
+
+            mx_tile(0)
+            mx_tile(1)
+            for m in range(MT):
+                if m + 2 < MT:
+                    mx_tile(m + 2)
+                finish_tile(m)

@@ -23,10 +23,11 @@ EPS = 1e-5
 FLOPS = 2 * ROWS * K * DOUT
 
 KB_V = 6
-N_ONES = 32
+N_S = KB - KB_V
+N_ONES = 256
 S_REGROUP = {0: (1, 2, 3), 1: (1, 2, 3), 2: (1, 2, 3), 3: (1, 3)}
-V_EVAC = (1, 4, 6)
 STORE_GROUPS = ((0, 1), (2, 3), (4, 5), (6,), (7,))
+LAG = 2
 
 
 def tile_settransform_pa_t_kernel(tc, set_feats, g0, b0, W0, c0, g1, b1, out):
@@ -39,8 +40,6 @@ def tile_settransform_pa_t_kernel(tc, set_feats, g0, b0, W0, c0, g1, b1, out):
         const = ctx.enter_context(tc.tile_pool(name="const", bufs=1))
         big = ctx.enter_context(tc.tile_pool(name="big", bufs=4))
         small = ctx.enter_context(tc.tile_pool(name="small", bufs=3))
-        ps_t = ctx.enter_context(tc.psum_pool(name="ps_t", bufs=4))
-        ps_m = ctx.enter_context(tc.psum_pool(name="ps_m", bufs=4))
 
         eps_t = const.tile([P, 1], F32, name="eps_t")
         nc.vector.memset(eps_t[:], EPS)
@@ -53,121 +52,124 @@ def tile_settransform_pa_t_kernel(tc, set_feats, g0, b0, W0, c0, g1, b1, out):
         make_identity(nc, ident_f[:])
         ones_bf = const.tile([P, N_ONES], BF16, name="ones_bf")
         nc.vector.memset(ones_bf[:], 1.0)
-
         praw = const.tile([P, P], BF16, name="praw")
         nc.vector.memset(praw[:], 0.0)
-        for i, v in enumerate((g0, b0, c0, g1, b1)):
-            nc.scalar.dma_start(out=praw[8 * i : 8 * i + 8, :], in_=v.rearrange("(j p) -> j p", p=P))
-        pps = ps_t.tile([P, P], BF16, name="pps", tag="tp")
-        nc.tensor.transpose(pps[:], praw[:], ident_bf[:])
-        par = const.tile([P, 40], F32, name="par")
-        nc.vector.tensor_copy(out=par[:], in_=pps[:, 0:40])
-        gpair = const.tile([P, MT, 2], F32, name="gpair")
-        nc.vector.tensor_copy(out=gpair[:, :, 0], in_=par[:, 24:32])
-        nc.vector.tensor_scalar(out=gpair[:, :, 1], in0=par[:, 24:32], scalar1=-1.0, scalar2=None, op0=ALU.mult)
 
+        par = const.tile([P, 40], F32, name="par")
+        gpair = const.tile([P, MT, 2], F32, name="gpair")
         xq = [const.tile([P, 2, 1024], U32, name="xq%d" % q, align_bytes=64) for q in range(4)]
         xsc = [const.tile([P, 2, 1024], U8, name="xsc%d" % q, align_bytes=64) for q in range(4)]
         wq = const.tile([P, 2, DOUT], U32, name="wq", align_bytes=64)
         wsc = const.tile([P, 2, DOUT], U8, name="wsc", align_bytes=64)
         st0 = const.tile([P, KB_V, 8, 6], F32, name="st0")
         mv0 = const.tile([P, KB, 2], F32, name="mv0")
-        n_s = KB - KB_V
-        nmu = const.tile([P, n_s], F32, name="nmu")
-        sq = const.tile([P, n_s, 4], F32, name="sq")
+        nmu = const.tile([P, N_S], F32, name="nmu")
+        sq = const.tile([P, N_S, 4], F32, name="sq")
+
+        ctx.enter_context(tc.manual_schedule())
 
         with ExitStack() as actx:
             xpool = actx.enter_context(tc.tile_pool(name="xpool", bufs=4))
             wpool = actx.enter_context(tc.tile_pool(name="wpool", bufs=1))
             gpool = actx.enter_context(tc.tile_pool(name="gpool", bufs=3))
             jpool = actx.enter_context(tc.tile_pool(name="jpool", bufs=2))
+            ps_a = actx.enter_context(tc.psum_pool(name="ps_a", bufs=5))
+            ps_s = actx.enter_context(tc.psum_pool(name="ps_s", bufs=1))
+
+            for i, v in enumerate((g0, b0, c0, g1, b1)):
+                nc.scalar.dma_start(out=praw[8 * i : 8 * i + 8, :], in_=v.rearrange("(j p) -> j p", p=P))
 
             xT = [big.tile([P, KB, 1024], BF16, name="xT%d" % q, tag="big") for q in range(4)]
             w_sb = wpool.tile([P, MT, K], BF16, name="w_sb")
-            wT = wpool.tile([P, KB, DOUT], BF16, name="wT")
             wg = wpool.tile([P, 2, DOUT, 4], BF16, name="wg", align_bytes=64)
-            sums = [ps_m.tile([P, N_ONES], F32, name="sums%d" % i, tag="acc") for i in range(n_s)]
-            first = ps_m.tile([P, n_s, N_ONES], F32, name="first", tag="acc")
+            sums = [ps_s.tile([P, N_ONES], F32, name="sums%d" % i) for i in range(N_S)]
+            first = ps_s.tile([P, N_S, 32], F32, name="first")
 
             def w_tile(m):
-                for hk in range(2):
-                    pt = ps_t.tile([P, 4, P], BF16, name="ptw", tag="tp")
+                for g in range(2):
+                    pt = ps_a.tile([P, 4, P], BF16, name="ptw", tag="tp")
                     for t in range(4):
-                        kb = 4 * hk + t
+                        kb = 4 * g + t
                         nc.tensor.transpose(pt[:, t, :], w_sb[:, m, kb * P : (kb + 1) * P], ident_bf[:])
-                    nc.scalar.copy(out=wT[:, 4 * hk : 4 * hk + 4, m * P : (m + 1) * P], in_=pt[:])
+                    nc.scalar.copy(out=wg[:, g, m * P : (m + 1) * P, :], in_=pt[:].rearrange("p t d -> p d t"))
 
             for c in range(8):
                 x_sb = xpool.tile([P, 4, K], BF16, name="x_sb", tag="x_sb")
-                nc.sync.dma_start(out=x_sb[:], in_=x_v[:, 4 * c : 4 * c + 4, :])
-                if c == 3:
+                if c == 0:
+                    for hk in range(2):
+                        nc.sync.dma_start(
+                            out=x_sb[:, :, hk * 512 : (hk + 1) * 512], in_=x_v[:, 0:4, hk * 512 : (hk + 1) * 512]
+                        )
+                else:
+                    nc.sync.dma_start(out=x_sb[:], in_=x_v[:, 4 * c : 4 * c + 4, :])
+                if c == 1:
                     nc.sync.dma_start(out=w_sb[:], in_=w_v)
                 base = (c % 2) * 512
                 if c == 0:
-                    for i in range(n_s):
+                    for i in range(N_S):
                         kb = KB_V + i
                         nc.tensor.matmul(
-                            out=first[:, i, :], lhsT=x_sb[:, 0, kb * P : (kb + 1) * P], rhs=ones_bf[:],
+                            out=first[:, i, :], lhsT=x_sb[:, 0, kb * P : (kb + 1) * P], rhs=ones_bf[:, 0:32],
                             start=True, stop=True,
                         )
                     nc.scalar.activation(out=nmu[:], in_=first[:, :, 0], func=ACT.Copy, scale=-1.0 / P)
                 for kb in range(KB):
-                    pt = ps_t.tile([P, 4, P], BF16, name="pt", tag="tp")
+                    pt = ps_a.tile([P, 4, P], BF16, name="pt", tag="tp")
                     for jj in range(4):
                         nc.tensor.transpose(pt[:, jj, :], x_sb[:, jj, kb * P : (kb + 1) * P], ident_bf[:])
+                    i, jj = kb // 4, kb % 4
+                    ks = KB_V + i
+                    nc.tensor.matmul(
+                        out=sums[i][:], lhsT=x_sb[:, jj, ks * P : (ks + 1) * P], rhs=ones_bf[:],
+                        start=(c == 0 and jj == 0), stop=(c == 7 and jj == 3),
+                    )
                     dst = xT[c // 2][:, kb, base : base + 512]
-                    nc.scalar.copy(out=dst, in_=pt[:].rearrange("p j r -> p (j r)"))
+                    src = pt[:].rearrange("p j r -> p (j r)")
+                    if kb == 0 or (kb == 1 and c % 2 == 1):
+                        nc.vector.tensor_copy(out=dst, in_=src)
+                    else:
+                        nc.scalar.copy(out=dst, in_=src)
                     if kb < KB_V:
                         nc.vector.bn_stats(out=st0[:, kb, c, :], in_=dst)
-                    else:
-                        for jj in range(4):
-                            nc.tensor.matmul(
-                                out=sums[kb - KB_V][:], lhsT=x_sb[:, jj, kb * P : (kb + 1) * P], rhs=ones_bf[:],
-                                start=(c == 0 and jj == 0), stop=(c == 7 and jj == 3),
-                            )
                 if c % 2 == 1:
-                    for i in range(n_s):
+                    for i in range(N_S):
                         junk = jpool.tile([P, 1024], BF16, name="junk", tag="junk")
                         nc.scalar.activation(
                             out=junk[:], in_=xT[c // 2][:, KB_V + i, :], func=ACT.Square,
                             bias=nmu[:, i : i + 1], scale=1.0, accum_out=sq[:, i, c // 2 : c // 2 + 1],
                         )
-                if c >= 4:
-                    w_tile(2 * (c - 4))
-                    w_tile(2 * (c - 4) + 1)
-                    if c % 2 == 1:
-                        lo = (c - 5) * 256
-                        for g in range(2):
-                            nc.gpsimd.tensor_scalar(
-                                out=wg[:, g, lo : lo + 512, :],
-                                in0=wT[:, 4 * g : 4 * g + 4, lo : lo + 512].rearrange("p t d -> p d t"),
-                                scalar1=1.0, scalar2=0.0, op0=ALU.mult, op1=ALU.add,
-                            )
-
-            for g in range(2):
-                nc.vector.quantize_mx(
-                    out=wq[:, g, :].bitcast(FP8X4),
-                    scales=wsc[:, g, :],
-                    in_=wg[:, g, :, :].rearrange("p d t -> p (d t)"),
-                )
+                if 3 <= c <= 6:
+                    w_tile(c - 3)
+                if c == 2:
+                    pps = ps_a.tile([P, P], BF16, name="pps", tag="tp")
+                    nc.tensor.transpose(pps[:], praw[:], ident_bf[:])
+                    nc.vector.tensor_copy(out=par[:], in_=pps[:, 0:40])
+                    nc.vector.tensor_copy(out=gpair[:, :, 0], in_=par[:, 24:32])
+                    nc.vector.tensor_scalar(
+                        out=gpair[:, :, 1], in0=par[:, 24:32], scalar1=-1.0, scalar2=None, op0=ALU.mult
+                    )
 
             for kb in range(KB_V):
                 nc.vector.bn_aggr(out=mv0[:, kb, :], in_=st0[:, kb, :, :].rearrange("p c s -> p (c s)"))
-            for i in range(n_s):
+            for i in range(N_S):
                 nc.vector.tensor_scalar(
                     out=mv0[:, KB_V + i, 0:1], in0=sums[i][:, 0:1], scalar1=1.0 / ROWS, scalar2=None, op0=ALU.mult
                 )
-            sqs = const.tile([P, n_s], F32, name="sqs")
+            sqs = const.tile([P, N_S], F32, name="sqs")
             nc.vector.tensor_reduce(out=sqs[:], in_=sq[:], axis=AX.X, op=ALU.add)
-            dl = const.tile([P, n_s], F32, name="dl")
+            dl = const.tile([P, N_S], F32, name="dl")
             nc.vector.tensor_tensor(out=dl[:], in0=mv0[:, KB_V:KB, 0], in1=nmu[:], op=ALU.add)
-            dl2 = const.tile([P, n_s], F32, name="dl2")
+            dl2 = const.tile([P, N_S], F32, name="dl2")
             nc.vector.tensor_tensor(out=dl2[:], in0=dl[:], in1=dl[:], op=ALU.mult)
             nc.vector.scalar_tensor_tensor(
                 out=mv0[:, KB_V:KB, 1], in0=sqs[:], scalar=1.0 / ROWS, in1=dl2[:], op0=ALU.mult, op1=ALU.subtract
             )
+            w_tile(4)
+            w_tile(5)
             sd0 = const.tile([P, KB], F32, name="sd0")
             nc.scalar.activation(out=sd0[:], in_=mv0[:, :, 1], func=ACT.Sqrt, bias=eps_t[:, 0:1], scale=1.0)
+            w_tile(6)
+            w_tile(7)
             r0 = const.tile([P, KB], F32, name="r0")
             nc.vector.reciprocal(out=r0[:], in_=sd0[:])
             a0 = const.tile([P, KB], F32, name="a0")
@@ -177,15 +179,20 @@ def tile_settransform_pa_t_kernel(tc, set_feats, g0, b0, W0, c0, g1, b1, out):
             nd0 = const.tile([P, KB], F32, name="nd0")
             nc.vector.tensor_tensor(out=nd0[:], in0=ma0[:], in1=par[:, 8:16], op=ALU.subtract)
 
-            for q in range(4):
+            def normalise_x(q):
                 for kb in range(KB):
                     nc.vector.tensor_scalar(
                         out=xT[q][:, kb, :], in0=xT[q][:, kb, :],
                         scalar1=a0[:, kb : kb + 1], scalar2=nd0[:, kb : kb + 1],
                         op0=ALU.mult, op1=ALU.subtract,
                     )
+
+            normalise_x(0)
+            for q in range(4):
+                grs = []
                 for g in range(2):
                     gr = gpool.tile([P, 1024, 4], BF16, name="gr", tag="gr", align_bytes=64)
+                    grs.append(gr)
                     for hf in range(2):
                         src = xT[q][:, 4 * g : 4 * g + 4, hf * 512 : (hf + 1) * 512]
                         dst = gr[:, hf * 512 : (hf + 1) * 512, :]
@@ -195,23 +202,38 @@ def tile_settransform_pa_t_kernel(tc, set_feats, g0, b0, W0, c0, g1, b1, out):
                             nc.scalar.copy(out=dst_v, in_=src_v)
                         else:
                             nc.vector.tensor_copy(out=dst_v, in_=src_v)
+                if q + 1 < 4:
+                    normalise_x(q + 1)
+                if q == 0:
+                    for g in range(2):
+                        nc.vector.quantize_mx(
+                            out=wq[:, g, :].bitcast(FP8X4),
+                            scales=wsc[:, g, :],
+                            in_=wg[:, g, :, :].rearrange("p d t -> p (d t)"),
+                        )
+                for g in range(2):
                     nc.vector.quantize_mx(
                         out=xq[q][:, g, :].bitcast(FP8X4),
                         scales=xsc[q][:, g, :],
-                        in_=gr[:].rearrange("p r t -> p (r t)"),
+                        in_=grs[g][:].rearrange("p r t -> p (r t)"),
                     )
 
         with ExitStack() as bctx:
             spool = bctx.enter_context(tc.tile_pool(name="spool", bufs=2))
+            ps_t = bctx.enter_context(tc.psum_pool(name="ps_t", bufs=4))
+            ps_m = bctx.enter_context(tc.psum_pool(name="ps_m", bufs=4))
             h = {}
             st1 = {}
             stage = {}
 
-            def mx_tile(m):
-                h[m] = big.tile([P, ROWS], F32, name="h%d" % m, tag="big")
-                st1[m] = small.tile([P, 8, 6], F32, name="st1", tag="st1")
-                for c in range(8):
+            def mx_burst(m, half):
+                if half == 0:
+                    h[m] = big.tile([P, ROWS], F32, name="h%d" % m, tag="big")
+                    st1[m] = small.tile([P, 8, 6], F32, name="st1", tag="st1")
+                accs = []
+                for c in range(4 * half, 4 * half + 4):
                     acc = ps_m.tile([P, 512], F32, name="acc", tag="acc")
+                    accs.append(acc)
                     q, hf = c // 2, c % 2
                     for g in range(2):
                         nc.tensor.matmul_mx(
@@ -223,57 +245,84 @@ def tile_settransform_pa_t_kernel(tc, set_feats, g0, b0, W0, c0, g1, b1, out):
                             start=(g == 0),
                             stop=(g == 1),
                         )
+                for n, acc in enumerate(accs):
+                    c = 4 * half + n
                     nc.scalar.activation(
                         out=h[m][:, c * 512 : (c + 1) * 512], in_=acc[:], func=ACT.Relu,
                         bias=par[:, 16 + m : 17 + m], scale=1.0,
                     )
                     nc.vector.bn_stats(out=st1[m][:, c, :], in_=h[m][:, c * 512 : (c + 1) * 512])
 
-            def finish_tile(m):
-                mv = small.tile([P, 2], F32, name="mv", tag="mv")
-                nc.vector.bn_aggr(out=mv[:], in_=st1[m][:].rearrange("p c s -> p (c s)"))
-                sd = small.tile([P, 1], F32, name="sd", tag="sd")
-                nc.scalar.activation(out=sd[:], in_=mv[:, 1:2], func=ACT.Sqrt, bias=eps_t[:, 0:1], scale=1.0)
-                r1 = small.tile([P, 1], F32, name="r1", tag="r1")
-                nc.vector.reciprocal(out=r1[:], in_=sd[:])
-                a1 = small.tile([P, 2], F32, name="a1", tag="a1")
-                nc.vector.tensor_scalar(out=a1[:], in0=gpair[:, m, :], scalar1=r1[:, 0:1], scalar2=None, op0=ALU.mult)
-                d1 = small.tile([P, 1], F32, name="d1", tag="d1")
-                nc.vector.scalar_tensor_tensor(
-                    out=d1[:], in0=mv[:, 0:1], scalar=a1[:, 1:2], in1=par[:, 32 + m : 33 + m],
-                    op0=ALU.mult, op1=ALU.add,
-                )
-                for s in range(4):
-                    nc.gpsimd.tensor_scalar(
-                        out=h[m][:, s * 1024 : (s + 1) * 1024], in0=h[m][:, s * 1024 : (s + 1) * 1024],
-                        scalar1=a1[:, 0:1], scalar2=d1[:, 0:1], op0=ALU.mult, op1=ALU.add,
-                    )
-                grp = [gr_ for gr_ in STORE_GROUPS if m in gr_][0]
-                gi = grp.index(m)
-                width = len(grp) * P
-                if gi == 0:
-                    stage[grp] = spool.tile([P, RT, width], F32, name="stage", tag="stage")
-                stg = stage[grp]
-                for c in range(8):
+            def t_burst(m, half):
+                banks = []
+                for c in range(4 * half, 4 * half + 4):
                     pt = ps_t.tile([P, 4, P], F32, name="pto", tag="tp")
+                    banks.append(pt)
                     for jj in range(4):
                         j = 4 * c + jj
                         nc.tensor.transpose(pt[:, jj, :], h[m][:, j * P : (j + 1) * P], ident_f[:])
-                    dst = stg[:, 4 * c : 4 * c + 4, gi * P : (gi + 1) * P]
-                    if c in V_EVAC:
-                        nc.vector.tensor_copy(out=dst, in_=pt[:])
-                    else:
-                        nc.scalar.copy(out=dst, in_=pt[:])
-                    if gi == len(grp) - 1 and c % 2 == 1:
-                        s = c // 2
-                        nc.sync.dma_start(
-                            out=out_v[:, 8 * s : 8 * s + 8, grp[0] * P : grp[0] * P + width],
-                            in_=stg[:, 8 * s : 8 * s + 8, :],
-                        )
+                return banks
 
-            mx_tile(0)
-            mx_tile(1)
-            for m in range(MT):
-                if m + 2 < MT:
-                    mx_tile(m + 2)
-                finish_tile(m)
+            def evac(m, c, pt, on_vector):
+                grp = [gr_ for gr_ in STORE_GROUPS if m in gr_][0]
+                gi = grp.index(m)
+                width = len(grp) * P
+                if gi == 0 and c == 0:
+                    stage[grp] = spool.tile([P, RT, width], F32, name="stage", tag="stage")
+                stg = stage[grp]
+                dst = stg[:, 4 * c : 4 * c + 4, gi * P : (gi + 1) * P]
+                if on_vector:
+                    nc.vector.tensor_copy(out=dst, in_=pt[:])
+                else:
+                    nc.scalar.copy(out=dst, in_=pt[:])
+                if gi == len(grp) - 1 and c % 2 == 1:
+                    s = c // 2
+                    nc.sync.dma_start(
+                        out=out_v[:, 8 * s : 8 * s + 8, grp[0] * P : grp[0] * P + width],
+                        in_=stg[:, 8 * s : 8 * s + 8, :],
+                    )
+
+            for step in range(2 * (MT + LAG)):
+                m, half = step // 2, step % 2
+                mt = m - LAG
+                close = m < MT and half == 1
+                if m < MT:
+                    mx_burst(m, half)
+                if close:
+                    mv = small.tile([P, 2], F32, name="mv", tag="mv")
+                    nc.vector.bn_aggr(out=mv[:], in_=st1[m][:].rearrange("p c s -> p (c s)"))
+                banks = t_burst(mt, half) if mt >= 0 else []
+                if banks:
+                    evac(mt, 4 * half, banks[0], False)
+                    evac(mt, 4 * half + 1, banks[1], True)
+                if close:
+                    sd = small.tile([P, 1], F32, name="sd", tag="sd")
+                    nc.scalar.activation(out=sd[:], in_=mv[:, 1:2], func=ACT.Sqrt, bias=eps_t[:, 0:1], scale=1.0)
+                    r1 = small.tile([P, 1], F32, name="r1", tag="r1")
+                    nc.vector.reciprocal(out=r1[:], in_=sd[:])
+                    a1 = small.tile([P, 2], F32, name="a1", tag="a1")
+                    nc.vector.tensor_scalar(
+                        out=a1[:], in0=gpair[:, m, :], scalar1=r1[:, 0:1], scalar2=None, op0=ALU.mult
+                    )
+                    d1 = small.tile([P, 1], F32, name="d1", tag="d1")
+                    nc.vector.scalar_tensor_tensor(
+                        out=d1[:], in0=mv[:, 0:1], scalar=a1[:, 1:2], in1=par[:, 32 + m : 33 + m],
+                        op0=ALU.mult, op1=ALU.add,
+                    )
+                    for s in range(4):
+                        hs = h[m][:, s * 1024 : (s + 1) * 1024]
+                        if m == MT - 1 and s == 2:
+                            nc.scalar.activation(
+                                out=hs, in_=hs, func=ACT.Identity, bias=d1[:, 0:1], scale=a1[:, 0:1]
+                            )
+                        elif m == MT - 1 and s == 3:
+                            nc.vector.tensor_scalar(
+                                out=hs, in0=hs, scalar1=a1[:, 0:1], scalar2=d1[:, 0:1], op0=ALU.mult, op1=ALU.add
+                            )
+                        else:
+                            nc.gpsimd.tensor_scalar(
+                                out=hs, in0=hs, scalar1=a1[:, 0:1], scalar2=d1[:, 0:1], op0=ALU.mult, op1=ALU.add
+                            )
+                if banks:
+                    evac(mt, 4 * half + 2, banks[2], False)
+                    evac(mt, 4 * half + 3, banks[3], True)

@@ -22,12 +22,12 @@ MT = DOUT // P
 EPS = 1e-5
 FLOPS = 2 * ROWS * K * DOUT
 
-KB_V = 6
-N_S = KB - KB_V
+N_S = 2
+KB_V = KB - N_S
 N_ONES = 256
 S_REGROUP = {0: (1, 2, 3), 1: (1, 2, 3), 2: (1, 2, 3), 3: (1, 3)}
 STORE_GROUPS = ((0, 1), (2, 3), (4, 5), (6,), (7,))
-LAG = 2
+LAG = 3
 
 
 def tile_settransform_pa_t_kernel(tc, set_feats, g0, b0, W0, c0, g1, b1, out):
@@ -107,9 +107,8 @@ def tile_settransform_pa_t_kernel(tc, set_feats, g0, b0, W0, c0, g1, b1, out):
                 base = (c % 2) * 512
                 if c == 0:
                     for i in range(N_S):
-                        kb = KB_V + i
                         nc.tensor.matmul(
-                            out=first[:, i, :], lhsT=x_sb[:, 0, kb * P : (kb + 1) * P], rhs=ones_bf[:, 0:32],
+                            out=first[:, i, :], lhsT=x_sb[:, 0, i * P : (i + 1) * P], rhs=ones_bf[:, 0:32],
                             start=True, stop=True,
                         )
                     nc.scalar.activation(out=nmu[:], in_=first[:, :, 0], func=ACT.Copy, scale=-1.0 / P)
@@ -118,24 +117,23 @@ def tile_settransform_pa_t_kernel(tc, set_feats, g0, b0, W0, c0, g1, b1, out):
                     for jj in range(4):
                         nc.tensor.transpose(pt[:, jj, :], x_sb[:, jj, kb * P : (kb + 1) * P], ident_bf[:])
                     i, jj = kb // 4, kb % 4
-                    ks = KB_V + i
                     nc.tensor.matmul(
-                        out=sums[i][:], lhsT=x_sb[:, jj, ks * P : (ks + 1) * P], rhs=ones_bf[:],
+                        out=sums[i][:], lhsT=x_sb[:, jj, i * P : (i + 1) * P], rhs=ones_bf[:],
                         start=(c == 0 and jj == 0), stop=(c == 7 and jj == 3),
                     )
                     dst = xT[c // 2][:, kb, base : base + 512]
                     src = pt[:].rearrange("p j r -> p (j r)")
-                    if kb == 0 or (kb == 1 and c % 2 == 1):
+                    if kb == 2 or (kb == 3 and c % 2 == 1):
                         nc.vector.tensor_copy(out=dst, in_=src)
                     else:
                         nc.scalar.copy(out=dst, in_=src)
-                    if kb < KB_V:
-                        nc.vector.bn_stats(out=st0[:, kb, c, :], in_=dst)
+                    if kb >= N_S:
+                        nc.vector.bn_stats(out=st0[:, kb - N_S, c, :], in_=dst)
                 if c % 2 == 1:
                     for i in range(N_S):
                         junk = jpool.tile([P, 1024], BF16, name="junk", tag="junk")
                         nc.scalar.activation(
-                            out=junk[:], in_=xT[c // 2][:, KB_V + i, :], func=ACT.Square,
+                            out=junk[:], in_=xT[c // 2][:, i, :], func=ACT.Square,
                             bias=nmu[:, i : i + 1], scale=1.0, accum_out=sq[:, i, c // 2 : c // 2 + 1],
                         )
                 if 3 <= c <= 6:
@@ -149,20 +147,20 @@ def tile_settransform_pa_t_kernel(tc, set_feats, g0, b0, W0, c0, g1, b1, out):
                         out=gpair[:, :, 1], in0=par[:, 24:32], scalar1=-1.0, scalar2=None, op0=ALU.mult
                     )
 
-            for kb in range(KB_V):
-                nc.vector.bn_aggr(out=mv0[:, kb, :], in_=st0[:, kb, :, :].rearrange("p c s -> p (c s)"))
+            for kb in range(N_S, KB):
+                nc.vector.bn_aggr(out=mv0[:, kb, :], in_=st0[:, kb - N_S, :, :].rearrange("p c s -> p (c s)"))
             for i in range(N_S):
                 nc.vector.tensor_scalar(
-                    out=mv0[:, KB_V + i, 0:1], in0=sums[i][:, 0:1], scalar1=1.0 / ROWS, scalar2=None, op0=ALU.mult
+                    out=mv0[:, i, 0:1], in0=sums[i][:, 0:1], scalar1=1.0 / ROWS, scalar2=None, op0=ALU.mult
                 )
             sqs = const.tile([P, N_S], F32, name="sqs")
             nc.vector.tensor_reduce(out=sqs[:], in_=sq[:], axis=AX.X, op=ALU.add)
             dl = const.tile([P, N_S], F32, name="dl")
-            nc.vector.tensor_tensor(out=dl[:], in0=mv0[:, KB_V:KB, 0], in1=nmu[:], op=ALU.add)
+            nc.vector.tensor_tensor(out=dl[:], in0=mv0[:, 0:N_S, 0], in1=nmu[:], op=ALU.add)
             dl2 = const.tile([P, N_S], F32, name="dl2")
             nc.vector.tensor_tensor(out=dl2[:], in0=dl[:], in1=dl[:], op=ALU.mult)
             nc.vector.scalar_tensor_tensor(
-                out=mv0[:, KB_V:KB, 1], in0=sqs[:], scalar=1.0 / ROWS, in1=dl2[:], op0=ALU.mult, op1=ALU.subtract
+                out=mv0[:, 0:N_S, 1], in0=sqs[:], scalar=1.0 / ROWS, in1=dl2[:], op0=ALU.mult, op1=ALU.subtract
             )
             w_tile(4)
             w_tile(5)
@@ -253,10 +251,13 @@ def tile_settransform_pa_t_kernel(tc, set_feats, g0, b0, W0, c0, g1, b1, out):
                     )
                     nc.vector.bn_stats(out=st1[m][:, c, :], in_=h[m][:, c * 512 : (c + 1) * 512])
 
-            def t_burst(m, half):
+            def t_burst(m, half, spare):
                 banks = []
                 for c in range(4 * half, 4 * half + 4):
-                    pt = ps_t.tile([P, 4, P], F32, name="pto", tag="tp")
+                    if spare:
+                        pt = ps_m.tile([P, 4, P], F32, name="pts", tag="acc")
+                    else:
+                        pt = ps_t.tile([P, 4, P], F32, name="pto", tag="tp")
                     banks.append(pt)
                     for jj in range(4):
                         j = 4 * c + jj
@@ -282,19 +283,19 @@ def tile_settransform_pa_t_kernel(tc, set_feats, g0, b0, W0, c0, g1, b1, out):
                         in_=stg[:, 8 * s : 8 * s + 8, :],
                     )
 
-            for step in range(2 * (MT + LAG)):
+            for step in range(2 * MT + LAG):
                 m, half = step // 2, step % 2
-                mt = m - LAG
+                mt, th = (step - LAG) // 2, (step - LAG) % 2
                 close = m < MT and half == 1
                 if m < MT:
                     mx_burst(m, half)
                 if close:
                     mv = small.tile([P, 2], F32, name="mv", tag="mv")
                     nc.vector.bn_aggr(out=mv[:], in_=st1[m][:].rearrange("p c s -> p (c s)"))
-                banks = t_burst(mt, half) if mt >= 0 else []
+                banks = t_burst(mt, th, step == 2 * MT + 1) if step >= LAG else []
                 if banks:
-                    evac(mt, 4 * half, banks[0], False)
-                    evac(mt, 4 * half + 1, banks[1], True)
+                    evac(mt, 4 * th, banks[0], False)
+                    evac(mt, 4 * th + 1, banks[1], True)
                 if close:
                     sd = small.tile([P, 1], F32, name="sd", tag="sd")
                     nc.scalar.activation(out=sd[:], in_=mv[:, 1:2], func=ACT.Sqrt, bias=eps_t[:, 0:1], scale=1.0)
@@ -311,11 +312,11 @@ def tile_settransform_pa_t_kernel(tc, set_feats, g0, b0, W0, c0, g1, b1, out):
                     )
                     for s in range(4):
                         hs = h[m][:, s * 1024 : (s + 1) * 1024]
-                        if m == MT - 1 and s == 2:
+                        if m == MT - 1 and s == 1:
                             nc.scalar.activation(
                                 out=hs, in_=hs, func=ACT.Identity, bias=d1[:, 0:1], scale=a1[:, 0:1]
                             )
-                        elif m == MT - 1 and s == 3:
+                        elif m == MT - 1 and s == 0:
                             nc.vector.tensor_scalar(
                                 out=hs, in0=hs, scalar1=a1[:, 0:1], scalar2=d1[:, 0:1], op0=ALU.mult, op1=ALU.add
                             )
@@ -324,5 +325,5 @@ def tile_settransform_pa_t_kernel(tc, set_feats, g0, b0, W0, c0, g1, b1, out):
                                 out=hs, in0=hs, scalar1=a1[:, 0:1], scalar2=d1[:, 0:1], op0=ALU.mult, op1=ALU.add
                             )
                 if banks:
-                    evac(mt, 4 * half + 2, banks[2], False)
-                    evac(mt, 4 * half + 3, banks[3], True)
+                    evac(mt, 4 * th + 2, banks[2], False)
+                    evac(mt, 4 * th + 3, banks[3], th == 0 or m >= MT)

@@ -26,7 +26,7 @@ N_S = 2
 KB_V = KB - N_S
 N_ONES = 256
 S_REGROUP = {0: (1, 2, 3), 1: (1, 2, 3), 2: (1, 2, 3), 3: (1, 3)}
-STORE_GROUPS = ((0, 1), (2, 3), (4, 5), (6,), (7,))
+STORE_GROUPS = ((0, 1), (2, 3), (4,), (5,), (6,), (7,))
 LAG = 3
 
 
@@ -64,7 +64,7 @@ def tile_settransform_pa_t_kernel(tc, set_feats, g0, b0, W0, c0, g1, b1, out):
         st0 = const.tile([P, KB_V, 8, 6], F32, name="st0")
         mv0 = const.tile([P, KB, 2], F32, name="mv0")
         nmu = const.tile([P, N_S], F32, name="nmu")
-        sq = const.tile([P, N_S, 4], F32, name="sq")
+        sq = const.tile([P, N_S, 8], F32, name="sq")
 
         ctx.enter_context(tc.manual_schedule())
 
@@ -73,7 +73,7 @@ def tile_settransform_pa_t_kernel(tc, set_feats, g0, b0, W0, c0, g1, b1, out):
             wpool = actx.enter_context(tc.tile_pool(name="wpool", bufs=1))
             gpool = actx.enter_context(tc.tile_pool(name="gpool", bufs=3))
             jpool = actx.enter_context(tc.tile_pool(name="jpool", bufs=2))
-            ps_a = actx.enter_context(tc.psum_pool(name="ps_a", bufs=5))
+            ps_a = actx.enter_context(tc.psum_pool(name="ps_a", bufs=6))
             ps_s = actx.enter_context(tc.psum_pool(name="ps_s", bufs=1))
 
             for i, v in enumerate((g0, b0, c0, g1, b1)):
@@ -83,7 +83,7 @@ def tile_settransform_pa_t_kernel(tc, set_feats, g0, b0, W0, c0, g1, b1, out):
             w_sb = wpool.tile([P, MT, K], BF16, name="w_sb")
             wg = wpool.tile([P, 2, DOUT, 4], BF16, name="wg", align_bytes=64)
             sums = [ps_s.tile([P, N_ONES], F32, name="sums%d" % i) for i in range(N_S)]
-            first = ps_s.tile([P, N_S, 32], F32, name="first")
+            first = ps_a.tile([P, N_S, 32], F32, name="first", tag="tp")
 
             def w_tile(m):
                 for g in range(2):
@@ -102,7 +102,7 @@ def tile_settransform_pa_t_kernel(tc, set_feats, g0, b0, W0, c0, g1, b1, out):
                         )
                 else:
                     nc.sync.dma_start(out=x_sb[:], in_=x_v[:, 4 * c : 4 * c + 4, :])
-                if c == 1:
+                if c == 3:
                     nc.sync.dma_start(out=w_sb[:], in_=w_v)
                 base = (c % 2) * 512
                 if c == 0:
@@ -129,12 +129,12 @@ def tile_settransform_pa_t_kernel(tc, set_feats, g0, b0, W0, c0, g1, b1, out):
                         nc.scalar.copy(out=dst, in_=src)
                     if kb >= N_S:
                         nc.vector.bn_stats(out=st0[:, kb - N_S, c, :], in_=dst)
-                if c % 2 == 1:
-                    for i in range(N_S):
-                        junk = jpool.tile([P, 1024], BF16, name="junk", tag="junk")
+                    if kb in (3, 6):
+                        i = kb // 3 - 1
+                        junk = jpool.tile([P, 512], BF16, name="junk", tag="junk")
                         nc.scalar.activation(
-                            out=junk[:], in_=xT[c // 2][:, i, :], func=ACT.Square,
-                            bias=nmu[:, i : i + 1], scale=1.0, accum_out=sq[:, i, c // 2 : c // 2 + 1],
+                            out=junk[:], in_=xT[c // 2][:, i, base : base + 512], func=ACT.Square,
+                            bias=nmu[:, i : i + 1], scale=1.0, accum_out=sq[:, i, c : c + 1],
                         )
                 if 3 <= c <= 6:
                     w_tile(c - 3)
@@ -326,4 +326,4 @@ def tile_settransform_pa_t_kernel(tc, set_feats, g0, b0, W0, c0, g1, b1, out):
                             )
                 if banks:
                     evac(mt, 4 * th + 2, banks[2], False)
-                    evac(mt, 4 * th + 3, banks[3], th == 0 or m >= MT)
+                    evac(mt, 4 * th + 3, banks[3], True)

@@ -26,7 +26,7 @@ N_S = 2
 KB_V = KB - N_S
 N_ONES = 256
 S_REGROUP = {0: (1, 2, 3), 1: (1, 2, 3), 2: (1, 2, 3), 3: (1, 3)}
-STORE_GROUPS = ((0, 1), (2, 3), (4,), (5,), (6,), (7,))
+STORE_GROUPS = ((0, 1), (2, 3), (4, 5), (6, 7))
 LAG = 3
 
 

@@ -26,7 +26,7 @@ N_S = 2
 KB_V = KB - N_S
 N_ONES = 256
 S_REGROUP = {0: (1, 2, 3), 1: (1, 2, 3), 2: (1, 2, 3), 3: (1, 3)}
-STORE_GROUPS = ((0, 1), (2, 3), (4, 5), (6, 7))
+STORE_GROUPS = ((0, 1), (2, 3), (4,), (5,), (6,), (7,))
 LAG = 3
 
 
@@ -283,7 +283,8 @@ def tile_settransform_pa_t_kernel(tc, set_feats, g0, b0, W0, c0, g1, b1, out):
                         in_=stg[:, 8 * s : 8 * s + 8, :],
                     )
 
-            for step in range(2 * MT + LAG):
+            for step2 in range(2 * (2 * MT + LAG)):
+                step = step2 % (2 * MT + LAG)
                 m, half = step // 2, step % 2
                 mt, th = (step - LAG) // 2, (step - LAG) % 2
                 close = m < MT and half == 1

from contextlib import ExitStack

import concourse.mybir as mybir
from concourse.masks import make_identity

F32 = mybir.dt.float32
BF16 = mybir.dt.bfloat16
U32 = mybir.dt.uint32
U8 = mybir.dt.uint8
FP8X4 = mybir.dt.float8_e4m3fn_x4
ACT = mybir.ActivationFunctionType
ALU = mybir.AluOpType
AX = mybir.AxisListType

P = 128
ROWS = 4096
K = 1024
DOUT = 1024
RT = ROWS // P
KB = K // P
MT = DOUT // P
EPS = 1e-5
FLOPS = 2 * ROWS * K * DOUT

N_S = 2
KB_V = KB - N_S
N_ONES = 256
S_REGROUP = {0: (1, 2, 3), 1: (1, 2, 3), 2: (1, 2, 3), 3: (1, 3)}
STORE_GROUPS = ((0, 1), (2, 3), (4,), (5,), (6,), (7,))
LAG = 3


def tile_settransform_pa_t_kernel(tc, set_feats, g0, b0, W0, c0, g1, b1, out):
    nc = tc.nc
    x_v = set_feats.flatten_outer_dims().rearrange("(p j) k -> p j k", j=RT)
    out_v = out.flatten_outer_dims().rearrange("(p j) d -> p j d", j=RT)
    w_v = W0.rearrange("(m p) k -> p m k", p=P)

    with ExitStack() as ctx:
        const = ctx.enter_context(tc.tile_pool(name="const", bufs=1))
        big = ctx.enter_context(tc.tile_pool(name="big", bufs=4))
        small = ctx.enter_context(tc.tile_pool(name="small", bufs=3))

        eps_t = const.tile([P, 1], F32, name="eps_t")
        nc.vector.memset(eps_t[:], EPS)
        warm = const.tile([P, 1], F32, name="warm")
        nc.scalar.activation(out=warm[:], in_=eps_t[:], func=ACT.Sqrt)

        ident_bf = const.tile([P, P], BF16, name="ident_bf")
        make_identity(nc, ident_bf[:])
        ident_f = const.tile([P, P], F32, name="ident_f")
        make_identity(nc, ident_f[:])
        ones_bf = const.tile([P, N_ONES], BF16, name="ones_bf")
        nc.vector.memset(ones_bf[:], 1.0)
        praw = const.tile([P, P], BF16, name="praw")
        nc.vector.memset(praw[:], 0.0)

        par = const.tile([P, 40], F32, name="par")
        gpair = const.tile([P, MT, 2], F32, name="gpair")
        xq = [const.tile([P, 2, 1024], U32, name="xq%d" % q, align_bytes=64) for q in range(4)]
        xsc = [const.tile([P, 2, 1024], U8, name="xsc%d" % q, align_bytes=64) for q in range(4)]
        wq = const.tile([P, 2, DOUT], U32, name="wq", align_bytes=64)
        wsc = const.tile([P, 2, DOUT], U8, name="wsc", align_bytes=64)
        st0 = const.tile([P, KB_V, 8, 6], F32, name="st0")
        mv0 = const.tile([P, KB, 2], F32, name="mv0")
        nmu = const.tile([P, N_S], F32, name="nmu")
        sq = const.tile([P, N_S, 8], F32, name="sq")

        ctx.enter_context(tc.manual_schedule())

        with ExitStack() as actx:
            xpool = actx.enter_context(tc.tile_pool(name="xpool", bufs=4))
            wpool = actx.enter_context(tc.tile_pool(name="wpool", bufs=1))
            gpool = actx.enter_context(tc.tile_pool(name="gpool", bufs=3))
            jpool = actx.enter_context(tc.tile_pool(name="jpool", bufs=2))
            ps_a = actx.enter_context(tc.psum_pool(name="ps_a", bufs=6))
            ps_s = actx.enter_context(tc.psum_pool(name="ps_s", bufs=1))

            for i, v in enumerate((g0, b0, c0, g1, b1)):
                nc.scalar.dma_start(out=praw[8 * i : 8 * i + 8, :], in_=v.rearrange("(j p) -> j p", p=P))

            xT = [big.tile([P, KB, 1024], BF16, name="xT%d" % q, tag="big") for q in range(4)]
            w_sb = wpool.tile([P, MT, K], BF16, name="w_sb")
            wg = wpool.tile([P, 2, DOUT, 4], BF16, name="wg", align_bytes=64)
            sums = [ps_s.tile([P, N_ONES], F32, name="sums%d" % i) for i in range(N_S)]
            first = ps_a.tile([P, N_S, 32], F32, name="first", tag="tp")

            def w_tile(m):
                for g in range(2):
                    pt = ps_a.tile([P, 4, P], BF16, name="ptw", tag="tp")
                    for t in range(4):
                        kb = 4 * g + t
                        nc.tensor.transpose(pt[:, t, :], w_sb[:, m, kb * P : (kb + 1) * P], ident_bf[:])
                    nc.scalar.copy(out=wg[:, g, m * P : (m + 1) * P, :], in_=pt[:].rearrange("p t d -> p d t"))

            for c in range(8):
                x_sb = xpool.tile([P, 4, K], BF16, name="x_sb", tag="x_sb")
                if c == 0:
                    for hk in range(2):
                        nc.sync.dma_start(
                            out=x_sb[:, :, hk * 512 : (hk + 1) * 512], in_=x_v[:, 0:4, hk * 512 : (hk + 1) * 512]
                        )
                else:
                    nc.sync.dma_start(out=x_sb[:], in_=x_v[:, 4 * c : 4 * c + 4, :])
                if c == 3:
                    nc.sync.dma_start(out=w_sb[:], in_=w_v)
                base = (c % 2) * 512
                if c == 0:
                    for i in range(N_S):
                        nc.tensor.matmul(
                            out=first[:, i, :], lhsT=x_sb[:, 0, i * P : (i + 1) * P], rhs=ones_bf[:, 0:32],
                            start=True, stop=True,
                        )
                    nc.scalar.activation(out=nmu[:], in_=first[:, :, 0], func=ACT.Copy, scale=-1.0 / P)
                for kb in range(KB):
                    pt = ps_a.tile([P, 4, P], BF16, name="pt", tag="tp")
                    for jj in range(4):
                        nc.tensor.transpose(pt[:, jj, :], x_sb[:, jj, kb * P : (kb + 1) * P], ident_bf[:])
                    i, jj = kb // 4, kb % 4
                    nc.tensor.matmul(
                        out=sums[i][:], lhsT=x_sb[:, jj, i * P : (i + 1) * P], rhs=ones_bf[:],
                        start=(c == 0 and jj == 0), stop=(c == 7 and jj == 3),
                    )
                    dst = xT[c // 2][:, kb, base : base + 512]
                    src = pt[:].rearrange("p j r -> p (j r)")
                    if kb == 2 or (kb == 3 and c % 2 == 1):
                        nc.vector.tensor_copy(out=dst, in_=src)
                    else:
                        nc.scalar.copy(out=dst, in_=src)
                    if kb >= N_S:
                        nc.vector.bn_stats(out=st0[:, kb - N_S, c, :], in_=dst)
                    if kb in (3, 6):
                        i = kb // 3 - 1
                        junk = jpool.tile([P, 512], BF16, name="junk", tag="junk")
                        nc.scalar.activation(
                            out=junk[:], in_=xT[c // 2][:, i, base : base + 512], func=ACT.Square,
                            bias=nmu[:, i : i + 1], scale=1.0, accum_out=sq[:, i, c : c + 1],
                        )
                if 3 <= c <= 6:
                    w_tile(c - 3)
                if c == 2:
                    pps = ps_a.tile([P, P], BF16, name="pps", tag="tp")
                    nc.tensor.transpose(pps[:], praw[:], ident_bf[:])
                    nc.vector.tensor_copy(out=par[:], in_=pps[:, 0:40])
                    nc.vector.tensor_copy(out=gpair[:, :, 0], in_=par[:, 24:32])
                    nc.vector.tensor_scalar(
                        out=gpair[:, :, 1], in0=par[:, 24:32], scalar1=-1.0, scalar2=None, op0=ALU.mult
                    )

            for kb in range(N_S, KB):
                nc.vector.bn_aggr(out=mv0[:, kb, :], in_=st0[:, kb - N_S, :, :].rearrange("p c s -> p (c s)"))
            for i in range(N_S):
                nc.vector.tensor_scalar(
                    out=mv0[:, i, 0:1], in0=sums[i][:, 0:1], scalar1=1.0 / ROWS, scalar2=None, op0=ALU.mult
                )
            sqs = const.tile([P, N_S], F32, name="sqs")
            nc.vector.tensor_reduce(out=sqs[:], in_=sq[:], axis=AX.X, op=ALU.add)
            dl = const.tile([P, N_S], F32, name="dl")
            nc.vector.tensor_tensor(out=dl[:], in0=mv0[:, 0:N_S, 0], in1=nmu[:], op=ALU.add)
            dl2 = const.tile([P, N_S], F32, name="dl2")
            nc.vector.tensor_tensor(out=dl2[:], in0=dl[:], in1=dl[:], op=ALU.mult)
            nc.vector.scalar_tensor_tensor(
                out=mv0[:, 0:N_S, 1], in0=sqs[:], scalar=1.0 / ROWS, in1=dl2[:], op0=ALU.mult, op1=ALU.subtract
            )
            w_tile(4)
            w_tile(5)
            sd0 = const.tile([P, KB], F32, name="sd0")
            nc.scalar.activation(out=sd0[:], in_=mv0[:, :, 1], func=ACT.Sqrt, bias=eps_t[:, 0:1], scale=1.0)
            w_tile(6)
            w_tile(7)
            r0 = const.tile([P, KB], F32, name="r0")
            nc.vector.reciprocal(out=r0[:], in_=sd0[:])
            a0 = const.tile([P, KB], F32, name="a0")
            nc.vector.tensor_tensor(out=a0[:], in0=r0[:], in1=par[:, 0:8], op=ALU.mult)
            ma0 = const.tile([P, KB], F32, name="ma0")
            nc.vector.tensor_tensor(out=ma0[:], in0=mv0[:, :, 0], in1=a0[:], op=ALU.mult)
            nd0 = const.tile([P, KB], F32, name="nd0")
            nc.vector.tensor_tensor(out=nd0[:], in0=ma0[:], in1=par[:, 8:16], op=ALU.subtract)

            def normalise_x(q):
                for kb in range(KB):
                    nc.vector.tensor_scalar(
                        out=xT[q][:, kb, :], in0=xT[q][:, kb, :],
                        scalar1=a0[:, kb : kb + 1], scalar2=nd0[:, kb : kb + 1],
                        op0=ALU.mult, op1=ALU.subtract,
                    )

            normalise_x(0)
            for q in range(4):
                grs = []
                for g in range(2):
                    gr = gpool.tile([P, 1024, 4], BF16, name="gr", tag="gr", align_bytes=64)
                    grs.append(gr)
                    for hf in range(2):
                        src = xT[q][:, 4 * g : 4 * g + 4, hf * 512 : (hf + 1) * 512]
                        dst = gr[:, hf * 512 : (hf + 1) * 512, :]
                        dst_v = dst.rearrange("p (c i) t -> p c t i", i=4)
                        src_v = src.rearrange("p t (c i) -> p c t i", i=4)
                        if 2 * g + hf in S_REGROUP[q]:
                            nc.scalar.copy(out=dst_v, in_=src_v)
                        else:
                            nc.vector.tensor_copy(out=dst_v, in_=src_v)
                if q + 1 < 4:
                    normalise_x(q + 1)
                if q == 0:
                    for g in range(2):
                        nc.vector.quantize_mx(
                            out=wq[:, g, :].bitcast(FP8X4),
                            scales=wsc[:, g, :],
                            in_=wg[:, g, :, :].rearrange("p d t -> p (d t)"),
                        )
                for g in range(2):
                    nc.vector.quantize_mx(
                        out=xq[q][:, g, :].bitcast(FP8X4),
                        scales=xsc[q][:, g, :],
                        in_=grs[g][:].rearrange("p r t -> p (r t)"),
                    )

        with ExitStack() as bctx:
            spool = bctx.enter_context(tc.tile_pool(name="spool", bufs=2))
            ps_t = bctx.enter_context(tc.psum_pool(name="ps_t", bufs=4))
            ps_m = bctx.enter_context(tc.psum_pool(name="ps_m", bufs=4))
            h = {}
            st1 = {}
            stage = {}

            def mx_burst(m, half):
                if half == 0:
                    h[m] = big.tile([P, ROWS], F32, name="h%d" % m, tag="big")
                    st1[m] = small.tile([P, 8, 6], F32, name="st1", tag="st1")
                accs = []
                for c in range(4 * half, 4 * half + 4):
                    acc = ps_m.tile([P, 512], F32, name="acc", tag="acc")
                    accs.append(acc)
                    q, hf = c // 2, c % 2
                    for g in range(2):
                        nc.tensor.matmul_mx(
                            out=acc[:],
                            lhsT=wq[:, g, m * P : (m + 1) * P].bitcast(FP8X4),
                            lhsT_scale=wsc[:, g, m * P : (m + 1) * P],
                            rhs=xq[q][:, g, hf * 512 : (hf + 1) * 512].bitcast(FP8X4),
                            rhs_scale=xsc[q][:, g, hf * 512 : (hf + 1) * 512],
                            start=(g == 0),
                            stop=(g == 1),
                        )
                for n, acc in enumerate(accs):
                    c = 4 * half + n
                    nc.scalar.activation(
                        out=h[m][:, c * 512 : (c + 1) * 512], in_=acc[:], func=ACT.Relu,
                        bias=par[:, 16 + m : 17 + m], scale=1.0,
                    )
                    nc.vector.bn_stats(out=st1[m][:, c, :], in_=h[m][:, c * 512 : (c + 1) * 512])

            def t_burst(m, half, spare):
                banks = []
                for c in range(4 * half, 4 * half + 4):
                    if spare:
                        pt = ps_m.tile([P, 4, P], F32, name="pts", tag="acc")
                    else:
                        pt = ps_t.tile([P, 4, P], F32, name="pto", tag="tp")
                    banks.append(pt)
                    for jj in range(4):
                        j = 4 * c + jj
                        nc.tensor.transpose(pt[:, jj, :], h[m][:, j * P : (j + 1) * P], ident_f[:])
                return banks

            def evac(m, c, pt, on_vector):
                grp = [gr_ for gr_ in STORE_GROUPS if m in gr_][0]
                gi = grp.index(m)
                width = len(grp) * P
                if gi == 0 and c == 0:
                    stage[grp] = spool.tile([P, RT, width], F32, name="stage", tag="stage")
                stg = stage[grp]
                dst = stg[:, 4 * c : 4 * c + 4, gi * P : (gi + 1) * P]
                if on_vector:
                    nc.vector.tensor_copy(out=dst, in_=pt[:])
                else:
                    nc.scalar.copy(out=dst, in_=pt[:])
                if gi == len(grp) - 1 and c % 2 == 1:
                    s = c // 2
                    nc.sync.dma_start(
                        out=out_v[:, 8 * s : 8 * s + 8, grp[0] * P : grp[0] * P + width],
                        in_=stg[:, 8 * s : 8 * s + 8, :],
                    )

            for step2 in range(2 * (2 * MT + LAG)):
                step = step2 % (2 * MT + LAG)
                m, half = step // 2, step % 2
                mt, th = (step - LAG) // 2, (step - LAG) % 2
                close = m < MT and half == 1
                if m < MT:
                    mx_burst(m, half)
                if close:
                    mv = small.tile([P, 2], F32, name="mv", tag="mv")
                    nc.vector.bn_aggr(out=mv[:], in_=st1[m][:].rearrange("p c s -> p (c s)"))
                banks = t_burst(mt, th, step == 2 * MT + 1) if step >= LAG else []
                if banks:
                    evac(mt, 4 * th, banks[0], False)
                    evac(mt, 4 * th + 1, banks[1], True)
                if close:
                    sd = small.tile([P, 1], F32, name="sd", tag="sd")
                    nc.scalar.activation(out=sd[:], in_=mv[:, 1:2], func=ACT.Sqrt, bias=eps_t[:, 0:1], scale=1.0)
                    r1 = small.tile([P, 1], F32, name="r1", tag="r1")
                    nc.vector.reciprocal(out=r1[:], in_=sd[:])
                    a1 = small.tile([P, 2], F32, name="a1", tag="a1")
                    nc.vector.tensor_scalar(
                        out=a1[:], in0=gpair[:, m, :], scalar1=r1[:, 0:1], scalar2=None, op0=ALU.mult
                    )
                    d1 = small.tile([P, 1], F32, name="d1", tag="d1")
                    nc.vector.scalar_tensor_tensor(
                        out=d1[:], in0=mv[:, 0:1], scalar=a1[:, 1:2], in1=par[:, 32 + m : 33 + m],
                        op0=ALU.mult, op1=ALU.add,
                    )
                    for s in range(4):
                        hs = h[m][:, s * 1024 : (s + 1) * 1024]
                        if m == MT - 1 and s == 1:
                            nc.scalar.activation(
                                out=hs, in_=hs, func=ACT.Identity, bias=d1[:, 0:1], scale=a1[:, 0:1]
                            )
                        elif m == MT - 1 and s == 0:
                            nc.vector.tensor_scalar(
                                out=hs, in0=hs, scalar1=a1[:, 0:1], scalar2=d1[:, 0:1], op0=ALU.mult, op1=ALU.add
                            )
                        else:
                            nc.gpsimd.tensor_scalar(
                                out=hs, in0=hs, scalar1=a1[:, 0:1], scalar2=d1[:, 0:1], op0=ALU.mult, op1=ALU.add
                            )
                if banks:
                    evac(mt, 4 * th + 2, banks[2], False)
                    evac(mt, 4 * th + 3, banks[3], True)
